import numpy as np
import ml_dtypes


def mxq(x, axis, fmt="e4m3"):
    dtype, down = {"e4m3": (ml_dtypes.float8_e4m3fn, 7), "e5m2": (ml_dtypes.float8_e5m2, 14)}[fmt]
    v = np.moveaxis(np.asarray(x, np.float32).astype(ml_dtypes.bfloat16).astype(np.float64), axis, -1)
    blocks = v.reshape(v.shape[:-1] + (-1, 32))
    amax = np.abs(blocks).max(-1, keepdims=True)
    byte = np.maximum(np.where(amax > 0, np.frexp(amax)[1] - 1 + 127, 0) - down, 1)
    scale = np.exp2(byte - 127.0)
    codes = (blocks / scale).astype(np.float32).astype(dtype).astype(np.float64)
    return np.moveaxis((codes * scale).reshape(v.shape), -1, axis)


WIDE = False


def mx_kscale(k):
    if not WIDE:
        return np.ones(k)
    levels = np.array([10, -10, 5, -5, 0])
    a = np.random.permutation(np.resize(levels, k // 512 * 4)).reshape(k // 512, 4)
    idx = np.arange(k)
    return np.exp2(a[idx // 512, idx % 128 // 32])


BF16 = ml_dtypes.bfloat16


def bf(x):
    return np.asarray(x, np.float32).astype(BF16)


def f64(x):
    return np.asarray(x).astype(np.float64)


E2M1 = np.array([0.0, 0.5, 1.0, 1.5, 2.0, 3.0, 4.0, 6.0, -0.0, -0.5, -1.0, -1.5, -2.0, -3.0, -4.0, -6.0])


def pack_weight(w, fmt):
    k, n = w.shape
    w = f64(bf(w)).reshape(k // 32, 32, n)
    amax = np.abs(w).max(1)
    if fmt == "e4m3":
        byte = np.frexp(amax)[1] - 1 + 127 - 7
    else:
        mant, ex = np.frexp(amax / 6.0)
        byte = np.where(mant > 0.5, ex, ex - 1) + 127
    byte = np.clip(np.where(amax > 0, byte, 1), 1, 254)
    scaled = (w * np.exp2(127.0 - byte)[:, None, :]).reshape(k, n).astype(np.float32)
    by_word = np.ascontiguousarray(scaled.reshape(k // 512, 128, 4, n).transpose(0, 1, 3, 2))
    if fmt == "e4m3":
        words = by_word.astype(ml_dtypes.float8_e4m3fn).view(np.uint8)
    else:
        c = by_word.astype(ml_dtypes.float4_e2m1fn).view(np.uint8) & 0xF
        words = c[..., 0::2] | (c[..., 1::2] << 4)
    return np.ascontiguousarray(words), np.ascontiguousarray(byte.astype(np.uint8).reshape(k // 512, 16, n))


def unpack_weight(words, scales, fmt):
    g, p, n, _ = words.shape
    if fmt == "e4m3":
        vals = np.ascontiguousarray(words).view(ml_dtypes.float8_e4m3fn).astype(np.float64)
    else:
        nib = np.empty((g, p, n, 4), np.uint8)
        nib[..., 0::2] = words & 0xF
        nib[..., 1::2] = words >> 4
        vals = E2M1[nib]
    vals = vals * np.repeat(np.exp2(scales.astype(np.float64) - 127.0), 8, axis=1)[..., None]
    return vals.transpose(0, 1, 3, 2).reshape(g * 512, n)


B, D, U, G, KS = 1536, 1024, 128, 5, 8
GRID_RANGE = (-1.0, 1.0)


def silu(v):
    return v / (1.0 + np.exp(-v))


def setup_inputs():
    s = mx_kscale(D)
    r = s / s.max()
    x = bf(np.random.standard_normal((B, D)) * r)
    base_weight_words, base_weight_scales = pack_weight(np.random.standard_normal((D, U)) / np.sqrt(D) / r[:, None], "e4m3")
    spline_weight = bf(np.random.standard_normal((D, U, KS)) / np.sqrt(D))
    return {"x": x,
            "base_weight_words": base_weight_words,
            "base_weight_scales": base_weight_scales,
            "spline_weight": spline_weight}


def reference(x, base_weight_words, base_weight_scales, spline_weight):
    x = f64(x)
    base_out = silu(mxq(x, 1, "e4m3") @ unpack_weight(base_weight_words, base_weight_scales, "e4m3"))
    centers = np.linspace(GRID_RANGE[0], GRID_RANGE[1], G)
    dist = np.square(x[..., None] - centers)
    rbf = np.exp(-5.0 * dist)
    rq = mxq(rbf, 1, "e4m3")
    wq = mxq(f64(spline_weight)[:, :, :G], 0, "e4m3")
    spline_out = (rq.transpose(2, 0, 1) @ wq.transpose(2, 0, 1)).sum(0)
    return base_out + spline_out

@@ -1,0 +1,201 @@
+from contextlib import ExitStack
+
+import concourse.mybir as mybir
+from concourse.masks import make_identity
+
+F32 = mybir.dt.float32
+BF16 = mybir.dt.bfloat16
+I32 = mybir.dt.int32
+U32 = mybir.dt.uint32
+U8 = mybir.dt.uint8
+FP8X4 = mybir.dt.float8_e4m3fn_x4
+ACT = mybir.ActivationFunctionType
+ALU = mybir.AluOpType
+
+ROWS, FEATURES, UNITS, SLICES = 1536, 1024, 128, 8
+CENTRES = (-1.0, -0.5, 0.0, 0.5, 1.0)
+SHARPNESS = 5.0
+
+P = 128
+PACK = 4
+K_PASS = P * PACK
+PASSES = FEATURES // K_PASS
+PAIRS = PACK // 2
+
+TILES = 2
+BLOCK_ROWS = TILES * P
+BLOCKS = ROWS // BLOCK_ROWS
+TILE_WORDS = PASSES * P
+BLOCK_WORDS = TILES * TILE_WORDS
+BLOCK_COLS = BLOCK_WORDS * PACK
+
+SCALAR_SQUARES = 1
+
+FLOPS = 2 * ROWS * FEATURES * UNITS * (1 + len(CENTRES))
+BYTES = (
+    2 * ROWS * FEATURES
+    + FEATURES * UNITS
+    + FEATURES // 32 * UNITS
+    + 2 * FEATURES * UNITS * len(CENTRES)
+    + 4 * ROWS * UNITS
+)
+
+
+def tile_kandense_kernel(tc, x, base_weight_words, base_weight_scales, spline_weight, out):
+    nc = tc.nc
+    x_blocks = x.rearrange("(n p j) k -> n p j k", p=P, j=TILES)
+    out_blocks = out.rearrange("(n p j) u -> n p j u", p=P, j=TILES)
+
+    with ExitStack() as ctx:
+        keep = ctx.enter_context(tc.tile_pool(name="keep", bufs=1))
+        x_pool = ctx.enter_context(tc.tile_pool(name="x_pool", bufs=BLOCKS))
+        work = ctx.enter_context(tc.tile_pool(name="work", bufs=3))
+        coded = ctx.enter_context(tc.tile_pool(name="coded", bufs=8))
+        x_psum = ctx.enter_context(tc.psum_pool(name="x_psum", bufs=2))
+        sums = ctx.enter_context(tc.psum_pool(name="sums", bufs=2))
+
+        x_rows = []
+        for n in range(BLOCKS):
+            x_rows.append(x_pool.tile([P, TILES, FEATURES], BF16, name="x_rows"))
+        nc.sync.dma_start(out=x_rows[0][:], in_=x_blocks[0])
+
+        base_codes = keep.tile([P, PASSES, UNITS], U32, align_bytes=64)
+        for c in range(PASSES):
+            nc.sync.dma_start(
+                out=base_codes[:, c, :].bitcast(I32),
+                in_=base_weight_words[c].rearrange("p n t -> p (n t)").bitcast(I32),
+            )
+        base_scales = keep.tile([P, PASSES, UNITS], U8, align_bytes=64)
+        nc.vector.memset(base_scales[:].rearrange("p c n -> p (c n)").bitcast(I32), 0)
+        scale_rows = base_weight_scales.rearrange("c q n -> q c n")
+        for quadrant in range(4):
+            nc.sync.dma_start(
+                out=base_scales[32 * quadrant : 32 * quadrant + 4].bitcast(I32),
+                in_=scale_rows[4 * quadrant : 4 * quadrant + 4].bitcast(I32),
+            )
+
+        w_rows = keep.tile([P, PASSES, PACK, UNITS * SLICES], BF16)
+        nc.sync.dma_start(
+            out=w_rows[:],
+            in_=spline_weight.rearrange("(c p t) u s -> p c t (u s)", p=P, t=PACK),
+        )
+        for n in range(1, BLOCKS):
+            nc.sync.dma_start(out=x_rows[n][:], in_=x_blocks[n])
+
+        identity = keep.tile([P, P], F32)
+        make_identity(nc, identity[:])
+
+        w_grouped = keep.tile([P, len(CENTRES), PASSES, UNITS, PACK], BF16, align_bytes=64)
+        w_codes = keep.tile([P, len(CENTRES), PASSES, UNITS], U32, align_bytes=64)
+        w_scales = keep.tile([P, len(CENTRES), PASSES, UNITS], U8, align_bytes=64)
+        w_by_slice = w_rows[:].rearrange("p c t (u s) -> p s c u t", s=SLICES)
+        for g in range(len(CENTRES)):
+            nc.vector.tensor_copy(out=w_grouped[:, g], in_=w_by_slice[:, g])
+        for g in range(len(CENTRES)):
+            nc.vector.quantize_mx(
+                out=w_codes[:, g].rearrange("p c u -> p (c u)").bitcast(FP8X4),
+                scales=w_scales[:, g].rearrange("p c u -> p (c u)"),
+                in_=w_grouped[:, g].rearrange("p c u t -> p (c u t)"),
+            )
+
+        def quantise_block(values):
+            codes = coded.tile([P, TILES, PASSES, P], U32, align_bytes=64, name="codes")
+            scales = coded.tile([P, TILES, PASSES, P], U8, align_bytes=64, name="scales")
+            nc.vector.quantize_mx(
+                out=codes[:].rearrange("p j c r -> p (j c r)").bitcast(FP8X4),
+                scales=scales[:].rearrange("p j c r -> p (j c r)"),
+                in_=values,
+            )
+            return codes, scales
+
+        def multiply(acc, codes, scales, j, weight_codes, weight_scales, first, last):
+            for c in range(PASSES):
+                nc.tensor.matmul_mx(
+                    out=acc,
+                    lhsT=codes[:, j, c, :].bitcast(FP8X4),
+                    lhsT_scale=scales[:, j, c, :],
+                    rhs=weight_codes[:, c, :].bitcast(FP8X4),
+                    rhs_scale=weight_scales[:, c, :],
+                    start=(first and c == 0),
+                    stop=(last and c == PASSES - 1),
+                )
+
+        for n in range(BLOCKS):
+            x_words = x_rows[n][:].bitcast(F32)
+            x_grouped = work.tile([P, BLOCK_COLS], BF16, align_bytes=64)
+            for j in range(TILES):
+                x_bank = x_psum.tile([P, PASSES, P, PAIRS], F32)
+                for c in range(PASSES):
+                    first_word = c * K_PASS // 2
+                    for u in range(PAIRS):
+                        nc.tensor.transpose(
+                            x_bank[:, c, :, u],
+                            x_words[:, j, first_word + u : first_word + K_PASS // 2 : PAIRS],
+                            identity[:],
+                        )
+                nc.vector.tensor_copy(
+                    out=x_grouped[:, j * TILE_WORDS * PACK : (j + 1) * TILE_WORDS * PACK].bitcast(F32),
+                    in_=x_bank[:].rearrange("p c r u -> p (c r u)"),
+                )
+
+            x_codes, x_scales = quantise_block(x_grouped[:])
+            base_sum = sums.tile([P, TILES, UNITS], F32)
+            for j in range(TILES):
+                multiply(base_sum[:, j, :], x_codes, x_scales, j, base_codes, base_scales, True, True)
+            base_flat = base_sum[:].rearrange("p j u -> p (j u)")
+            tanh_half = work.tile([P, TILES * UNITS], F32)
+            nc.scalar.activation(out=tanh_half[:], in_=base_flat, func=ACT.Tanh, scale=0.5)
+            twice_silu = work.tile([P, TILES, UNITS], F32)
+            nc.vector.scalar_tensor_tensor(
+                out=twice_silu[:].rearrange("p j u -> p (j u)"),
+                in0=tanh_half[:],
+                scalar=1.0,
+                in1=base_flat,
+                op0=ALU.add,
+                op1=ALU.mult,
+            )
+
+            spline_sum = [sums.tile([P, UNITS], F32, name="spline_sum%d" % j) for j in range(TILES)]
+            for g, centre in enumerate(CENTRES):
+                distance = work.tile([P, BLOCK_COLS], F32)
+                if g < SCALAR_SQUARES:
+                    nc.scalar.activation(out=distance[:], in_=x_grouped[:], func=ACT.Square, bias=-centre)
+                    rest = 0.0
+                else:
+                    nc.vector.scalar_tensor_tensor(
+                        out=distance[:],
+                        in0=x_grouped[:],
+                        scalar=2.0 * centre,
+                        in1=x_grouped[:],
+                        op0=ALU.subtract,
+                        op1=ALU.mult,
+                    )
+                    rest = centre * centre
+                rbf = work.tile([P, BLOCK_COLS], BF16, align_bytes=64)
+                nc.scalar.activation(
+                    out=rbf[:], in_=distance[:], func=ACT.Exp, scale=-SHARPNESS, bias=-SHARPNESS * rest
+                )
+                rbf_codes, rbf_scales = quantise_block(rbf[:])
+                for j in range(TILES):
+                    multiply(
+                        spline_sum[j][:],
+                        rbf_codes,
+                        rbf_scales,
+                        j,
+                        w_codes[:, g],
+                        w_scales[:, g],
+                        g == 0,
+                        g == len(CENTRES) - 1,
+                    )
+
+            result = work.tile([P, TILES, UNITS], F32)
+            for j in range(TILES):
+                nc.vector.scalar_tensor_tensor(
+                    out=result[:, j, :],
+                    in0=twice_silu[:, j, :],
+                    scalar=0.5,
+                    in1=spline_sum[j][:],
+                    op0=ALU.mult,
+                    op1=ALU.add,
+                )
+            nc.sync.dma_start(out=out_blocks[n], in_=result[:])

@@ -14,6 +14,7 @@ ALU = mybir.AluOpType
 
 ROWS, FEATURES, UNITS, SLICES = 1536, 1024, 128, 8
 CENTRES = (-1.0, -0.5, 0.0, 0.5, 1.0)
+GROUPS = len(CENTRES)
 SHARPNESS = 5.0
 
 P = 128
@@ -23,20 +24,24 @@ PASSES = FEATURES // K_PASS
 PAIRS = PACK // 2
 
 TILES = 2
-BLOCK_ROWS = TILES * P
-BLOCKS = ROWS // BLOCK_ROWS
-TILE_WORDS = PASSES * P
-BLOCK_WORDS = TILES * TILE_WORDS
-BLOCK_COLS = BLOCK_WORDS * PACK
+BLOCKS = ROWS // (TILES * P)
+TILE_COLS = PASSES * P * PACK
+BLOCK_COLS = TILES * TILE_COLS
+TASKS = BLOCKS * GROUPS
 
-SCALAR_SQUARES = 1
+MIDDLE = 2
+assert CENTRES[MIDDLE] == 0.0
+SHARED = GROUPS - 1
 
-FLOPS = 2 * ROWS * FEATURES * UNITS * (1 + len(CENTRES))
+AHEAD = 2
+BEHIND = 2
+
+FLOPS = 2 * ROWS * FEATURES * UNITS * (1 + GROUPS)
 BYTES = (
     2 * ROWS * FEATURES
     + FEATURES * UNITS
     + FEATURES // 32 * UNITS
-    + 2 * FEATURES * UNITS * len(CENTRES)
+    + 2 * FEATURES * UNITS * GROUPS
     + 4 * ROWS * UNITS
 )
 
@@ -49,10 +54,14 @@ def tile_kandense_kernel(tc, x, base_weight_words, base_weight_scales, spline_we
     with ExitStack() as ctx:
         keep = ctx.enter_context(tc.tile_pool(name="keep", bufs=1))
         x_pool = ctx.enter_context(tc.tile_pool(name="x_pool", bufs=BLOCKS))
-        work = ctx.enter_context(tc.tile_pool(name="work", bufs=3))
-        coded = ctx.enter_context(tc.tile_pool(name="coded", bufs=8))
-        x_psum = ctx.enter_context(tc.psum_pool(name="x_psum", bufs=2))
-        sums = ctx.enter_context(tc.psum_pool(name="sums", bufs=2))
+        by_block = ctx.enter_context(tc.tile_pool(name="by_block", bufs=2))
+        distances = ctx.enter_context(tc.tile_pool(name="distances", bufs=AHEAD + 2))
+        early_distances = ctx.enter_context(tc.tile_pool(name="early_distances", bufs=2))
+        rbfs = ctx.enter_context(tc.tile_pool(name="rbfs", bufs=BEHIND + 2))
+        coded = ctx.enter_context(tc.tile_pool(name="coded", bufs=4))
+        x_psum = ctx.enter_context(tc.psum_pool(name="x_psum", bufs=2 * TILES))
+        sums = ctx.enter_context(tc.psum_pool(name="sums", bufs=1))
+        ctx.enter_context(tc.manual_schedule())
 
         x_rows = []
         for n in range(BLOCKS):
@@ -74,24 +83,30 @@ def tile_kandense_kernel(tc, x, base_weight_words, base_weight_scales, spline_we
                 in_=scale_rows[4 * quadrant : 4 * quadrant + 4].bitcast(I32),
             )
 
+        nc.sync.dma_start(out=x_rows[1][:], in_=x_blocks[1])
+
         w_rows = keep.tile([P, PASSES, PACK, UNITS * SLICES], BF16)
         nc.sync.dma_start(
             out=w_rows[:],
             in_=spline_weight.rearrange("(c p t) u s -> p c t (u s)", p=P, t=PACK),
         )
-        for n in range(1, BLOCKS):
+        for n in range(2, BLOCKS):
             nc.sync.dma_start(out=x_rows[n][:], in_=x_blocks[n])
 
         identity = keep.tile([P, P], F32)
         make_identity(nc, identity[:])
 
-        w_grouped = keep.tile([P, len(CENTRES), PASSES, UNITS, PACK], BF16, align_bytes=64)
-        w_codes = keep.tile([P, len(CENTRES), PASSES, UNITS], U32, align_bytes=64)
-        w_scales = keep.tile([P, len(CENTRES), PASSES, UNITS], U8, align_bytes=64)
+        w_grouped = keep.tile([P, GROUPS, PASSES, UNITS, PACK], BF16, align_bytes=64)
+        w_codes = keep.tile([P, GROUPS, PASSES, UNITS], U32, align_bytes=64)
+        w_scales = keep.tile([P, GROUPS, PASSES, UNITS], U8, align_bytes=64)
         w_by_slice = w_rows[:].rearrange("p c t (u s) -> p s c u t", s=SLICES)
-        for g in range(len(CENTRES)):
-            nc.vector.tensor_copy(out=w_grouped[:, g], in_=w_by_slice[:, g])
-        for g in range(len(CENTRES)):
+
+        def regroup_weight(g):
+            nc.gpsimd.tensor_scalar(
+                out=w_grouped[:, g], in0=w_by_slice[:, g], scalar1=1.0, scalar2=0.0, op0=ALU.mult, op1=ALU.add
+            )
+
+        def quantise_weight(g):
             nc.vector.quantize_mx(
                 out=w_codes[:, g].rearrange("p c u -> p (c u)").bitcast(FP8X4),
                 scales=w_scales[:, g].rearrange("p c u -> p (c u)"),
@@ -120,9 +135,12 @@ def tile_kandense_kernel(tc, x, base_weight_words, base_weight_scales, spline_we
                     stop=(last and c == PASSES - 1),
                 )
 
-        for n in range(BLOCKS):
+        x_banks, x_grouped, base_sum, tanh_half, twice_silu, spline_sum = {}, {}, {}, {}, {}, {}
+        distance, rbf = {}, {}
+
+        def transpose_block(n):
             x_words = x_rows[n][:].bitcast(F32)
-            x_grouped = work.tile([P, BLOCK_COLS], BF16, align_bytes=64)
+            x_banks[n] = []
             for j in range(TILES):
                 x_bank = x_psum.tile([P, PASSES, P, PAIRS], F32)
                 for c in range(PASSES):
@@ -133,69 +151,134 @@ def tile_kandense_kernel(tc, x, base_weight_words, base_weight_scales, spline_we
                             x_words[:, j, first_word + u : first_word + K_PASS // 2 : PAIRS],
                             identity[:],
                         )
-                nc.vector.tensor_copy(
-                    out=x_grouped[:, j * TILE_WORDS * PACK : (j + 1) * TILE_WORDS * PACK].bitcast(F32),
-                    in_=x_bank[:].rearrange("p c r u -> p (c r u)"),
-                )
+                x_banks[n].append(x_bank)
 
-            x_codes, x_scales = quantise_block(x_grouped[:])
-            base_sum = sums.tile([P, TILES, UNITS], F32)
+        def group_block(n):
+            x_grouped[n] = by_block.tile([P, BLOCK_COLS], BF16, align_bytes=64, name="x_grouped")
             for j in range(TILES):
-                multiply(base_sum[:, j, :], x_codes, x_scales, j, base_codes, base_scales, True, True)
-            base_flat = base_sum[:].rearrange("p j u -> p (j u)")
-            tanh_half = work.tile([P, TILES * UNITS], F32)
-            nc.scalar.activation(out=tanh_half[:], in_=base_flat, func=ACT.Tanh, scale=0.5)
-            twice_silu = work.tile([P, TILES, UNITS], F32)
+                nc.scalar.copy(
+                    out=x_grouped[n][:, j * TILE_COLS : (j + 1) * TILE_COLS].bitcast(F32),
+                    in_=x_banks[n][j][:].rearrange("p c r u -> p (c r u)"),
+                )
+            middle = early_distances.tile([P, BLOCK_COLS], F32)
+            nc.gpsimd.tensor_tensor(out=middle[:], in0=x_grouped[n][:], in1=x_grouped[n][:], op=ALU.mult)
+            distance[GROUPS * n + MIDDLE] = middle
+            shared = early_distances.tile([P, BLOCK_COLS], F32)
+            last_tile = slice((TILES - 1) * TILE_COLS, TILES * TILE_COLS)
+            shifted = early_distances.tile([P, TILE_COLS], F32)
+            nc.gpsimd.tensor_scalar(
+                out=shifted[:],
+                in0=x_grouped[n][:, last_tile],
+                scalar1=-2.0 * CENTRES[SHARED],
+                scalar2=1.0,
+                op0=ALU.add,
+                op1=ALU.mult,
+            )
+            nc.gpsimd.tensor_tensor(
+                out=shared[:, last_tile], in0=shifted[:], in1=x_grouped[n][:, last_tile], op=ALU.mult
+            )
+            distance[GROUPS * n + SHARED] = shared
+
+        def base_product(n):
+            x_codes, x_scales = quantise_block(x_grouped[n][:])
+            base_sum[n] = sums.tile([P, TILES, UNITS], F32, name="base_sum")
+            for j in range(TILES):
+                multiply(base_sum[n][:, j, :], x_codes, x_scales, j, base_codes, base_scales, True, True)
+
+        def tanh_block(n):
+            tanh_half[n] = by_block.tile([P, TILES * UNITS], F32, name="tanh_half")
+            nc.scalar.activation(
+                out=tanh_half[n][:], in_=base_sum[n][:].rearrange("p j u -> p (j u)"), func=ACT.Tanh, scale=0.5
+            )
+
+        def silu_block(n):
+            twice_silu[n] = by_block.tile([P, TILES, UNITS], F32, name="twice_silu")
             nc.vector.scalar_tensor_tensor(
-                out=twice_silu[:].rearrange("p j u -> p (j u)"),
-                in0=tanh_half[:],
+                out=twice_silu[n][:].rearrange("p j u -> p (j u)"),
+                in0=tanh_half[n][:],
                 scalar=1.0,
-                in1=base_flat,
+                in1=base_sum[n][:].rearrange("p j u -> p (j u)"),
                 op0=ALU.add,
                 op1=ALU.mult,
             )
 
-            spline_sum = [sums.tile([P, UNITS], F32, name="spline_sum%d" % j) for j in range(TILES)]
-            for g, centre in enumerate(CENTRES):
-                distance = work.tile([P, BLOCK_COLS], F32)
-                if g < SCALAR_SQUARES:
-                    nc.scalar.activation(out=distance[:], in_=x_grouped[:], func=ACT.Square, bias=-centre)
-                    rest = 0.0
-                else:
-                    nc.vector.scalar_tensor_tensor(
-                        out=distance[:],
-                        in0=x_grouped[:],
-                        scalar=2.0 * centre,
-                        in1=x_grouped[:],
-                        op0=ALU.subtract,
-                        op1=ALU.mult,
-                    )
-                    rest = centre * centre
-                rbf = work.tile([P, BLOCK_COLS], BF16, align_bytes=64)
-                nc.scalar.activation(
-                    out=rbf[:], in_=distance[:], func=ACT.Exp, scale=-SHARPNESS, bias=-SHARPNESS * rest
+        def squared_distance(task):
+            n, g = divmod(task, GROUPS)
+            if g == MIDDLE:
+                return
+            if g != SHARED:
+                distance[task] = distances.tile([P, BLOCK_COLS], F32, name="distance")
+            for j in range(TILES - 1 if g == SHARED else TILES):
+                cols = slice(j * TILE_COLS, (j + 1) * TILE_COLS)
+                nc.vector.scalar_tensor_tensor(
+                    out=distance[task][:, cols],
+                    in0=x_banks[n][j][:].rearrange("p c r u -> p (c r u)").bitcast(BF16),
+                    scalar=2.0 * CENTRES[g],
+                    in1=x_grouped[n][:, cols],
+                    op0=ALU.subtract,
+                    op1=ALU.mult,
                 )
-                rbf_codes, rbf_scales = quantise_block(rbf[:])
-                for j in range(TILES):
-                    multiply(
-                        spline_sum[j][:],
-                        rbf_codes,
-                        rbf_scales,
-                        j,
-                        w_codes[:, g],
-                        w_scales[:, g],
-                        g == 0,
-                        g == len(CENTRES) - 1,
-                    )
 
-            result = work.tile([P, TILES, UNITS], F32)
+        def exponential(task):
+            centre = CENTRES[task % GROUPS]
+            rbf[task] = rbfs.tile([P, BLOCK_COLS], BF16, align_bytes=64, name="rbf")
+            nc.scalar.activation(
+                out=rbf[task][:],
+                in_=distance[task][:],
+                func=ACT.Exp,
+                scale=-SHARPNESS,
+                bias=-SHARPNESS * centre * centre,
+            )
+
+        def product(task):
+            n, g = divmod(task, GROUPS)
+            if g == 0:
+                spline_sum[n] = [sums.tile([P, UNITS], F32, name="spline_sum%d" % j) for j in range(TILES)]
+            rbf_codes, rbf_scales = quantise_block(rbf[task][:])
+            for j in range(TILES):
+                multiply(
+                    spline_sum[n][j][:], rbf_codes, rbf_scales, j, w_codes[:, g], w_scales[:, g],
+                    g == 0, g == GROUPS - 1,
+                )
+
+        def finish_block(n):
+            result = by_block.tile([P, TILES, UNITS], F32)
             for j in range(TILES):
                 nc.vector.scalar_tensor_tensor(
                     out=result[:, j, :],
-                    in0=twice_silu[:, j, :],
+                    in0=twice_silu[n][:, j, :],
                     scalar=0.5,
-                    in1=spline_sum[j][:],
+                    in1=spline_sum[n][j][:],
                     op0=ALU.mult,
                     op1=ALU.add,
                 )
             nc.sync.dma_start(out=out_blocks[n], in_=result[:])
+
+        transpose_block(0)
+        group_block(0)
+        for g in range(GROUPS):
+            regroup_weight(g)
+        for step in range(TASKS + AHEAD + BEHIND + 1):
+            n, g = divmod(step, GROUPS)
+            if n + 1 < BLOCKS:
+                if g == 1:
+                    transpose_block(n + 1)
+                if g == 2:
+                    group_block(n + 1)
+            if step < TASKS:
+                squared_distance(step)
+                if g == 0:
+                    base_product(n)
+                if g == 2:
+                    tanh_block(n)
+                if g == 3:
+                    silu_block(n)
+            if 0 <= step - AHEAD < TASKS:
+                exponential(step - AHEAD)
+            ripe = step - AHEAD - BEHIND
+            if ripe > 0 and ripe % GROUPS == 0:
+                finish_block(ripe // GROUPS - 1)
+            if 0 <= ripe < GROUPS:
+                quantise_weight(ripe)
+            if 0 <= ripe < TASKS:
+                product(ripe)

@@ -29,9 +29,7 @@ TILE_COLS = PASSES * P * PACK
 BLOCK_COLS = TILES * TILE_COLS
 TASKS = BLOCKS * GROUPS
 
-MIDDLE = 2
-assert CENTRES[MIDDLE] == 0.0
-SHARED = GROUPS - 1
+SCALAR_SQUARES = 1
 
 AHEAD = 2
 BEHIND = 2
@@ -56,11 +54,10 @@ def tile_kandense_kernel(tc, x, base_weight_words, base_weight_scales, spline_we
         x_pool = ctx.enter_context(tc.tile_pool(name="x_pool", bufs=BLOCKS))
         by_block = ctx.enter_context(tc.tile_pool(name="by_block", bufs=2))
         distances = ctx.enter_context(tc.tile_pool(name="distances", bufs=AHEAD + 2))
-        early_distances = ctx.enter_context(tc.tile_pool(name="early_distances", bufs=2))
         rbfs = ctx.enter_context(tc.tile_pool(name="rbfs", bufs=BEHIND + 2))
         coded = ctx.enter_context(tc.tile_pool(name="coded", bufs=4))
-        x_psum = ctx.enter_context(tc.psum_pool(name="x_psum", bufs=2 * TILES))
-        sums = ctx.enter_context(tc.psum_pool(name="sums", bufs=1))
+        x_psum = ctx.enter_context(tc.psum_pool(name="x_psum", bufs=TILES))
+        sums = ctx.enter_context(tc.psum_pool(name="sums", bufs=2))
         ctx.enter_context(tc.manual_schedule())
 
         x_rows = []
@@ -102,9 +99,10 @@ def tile_kandense_kernel(tc, x, base_weight_words, base_weight_scales, spline_we
         w_by_slice = w_rows[:].rearrange("p c t (u s) -> p s c u t", s=SLICES)
 
         def regroup_weight(g):
-            nc.gpsimd.tensor_scalar(
-                out=w_grouped[:, g], in0=w_by_slice[:, g], scalar1=1.0, scalar2=0.0, op0=ALU.mult, op1=ALU.add
-            )
+            if g % 2 == 0:
+                nc.vector.tensor_copy(out=w_grouped[:, g], in_=w_by_slice[:, g])
+            else:
+                nc.scalar.copy(out=w_grouped[:, g], in_=w_by_slice[:, g])
 
         def quantise_weight(g):
             nc.vector.quantize_mx(
@@ -156,28 +154,12 @@ def tile_kandense_kernel(tc, x, base_weight_words, base_weight_scales, spline_we
         def group_block(n):
             x_grouped[n] = by_block.tile([P, BLOCK_COLS], BF16, align_bytes=64, name="x_grouped")
             for j in range(TILES):
-                nc.scalar.copy(
-                    out=x_grouped[n][:, j * TILE_COLS : (j + 1) * TILE_COLS].bitcast(F32),
-                    in_=x_banks[n][j][:].rearrange("p c r u -> p (c r u)"),
-                )
-            middle = early_distances.tile([P, BLOCK_COLS], F32)
-            nc.gpsimd.tensor_tensor(out=middle[:], in0=x_grouped[n][:], in1=x_grouped[n][:], op=ALU.mult)
-            distance[GROUPS * n + MIDDLE] = middle
-            shared = early_distances.tile([P, BLOCK_COLS], F32)
-            last_tile = slice((TILES - 1) * TILE_COLS, TILES * TILE_COLS)
-            shifted = early_distances.tile([P, TILE_COLS], F32)
-            nc.gpsimd.tensor_scalar(
-                out=shifted[:],
-                in0=x_grouped[n][:, last_tile],
-                scalar1=-2.0 * CENTRES[SHARED],
-                scalar2=1.0,
-                op0=ALU.add,
-                op1=ALU.mult,
-            )
-            nc.gpsimd.tensor_tensor(
-                out=shared[:, last_tile], in0=shifted[:], in1=x_grouped[n][:, last_tile], op=ALU.mult
-            )
-            distance[GROUPS * n + SHARED] = shared
+                words_out = x_grouped[n][:, j * TILE_COLS : (j + 1) * TILE_COLS].bitcast(F32)
+                words_in = x_banks[n][j][:].rearrange("p c r u -> p (c r u)")
+                if j % 2 == 0:
+                    nc.vector.tensor_copy(out=words_out, in_=words_in)
+                else:
+                    nc.scalar.copy(out=words_out, in_=words_in)
 
         def base_product(n):
             x_codes, x_scales = quantise_block(x_grouped[n][:])
@@ -204,30 +186,31 @@ def tile_kandense_kernel(tc, x, base_weight_words, base_weight_scales, spline_we
 
         def squared_distance(task):
             n, g = divmod(task, GROUPS)
-            if g == MIDDLE:
-                return
-            if g != SHARED:
-                distance[task] = distances.tile([P, BLOCK_COLS], F32, name="distance")
-            for j in range(TILES - 1 if g == SHARED else TILES):
-                cols = slice(j * TILE_COLS, (j + 1) * TILE_COLS)
+            distance[task] = distances.tile([P, BLOCK_COLS], F32, name="distance")
+            if g < SCALAR_SQUARES:
+                nc.scalar.activation(
+                    out=distance[task][:], in_=x_grouped[n][:], func=ACT.Square, bias=-CENTRES[g]
+                )
+            else:
                 nc.vector.scalar_tensor_tensor(
-                    out=distance[task][:, cols],
-                    in0=x_banks[n][j][:].rearrange("p c r u -> p (c r u)").bitcast(BF16),
+                    out=distance[task][:],
+                    in0=x_grouped[n][:],
                     scalar=2.0 * CENTRES[g],
-                    in1=x_grouped[n][:, cols],
+                    in1=x_grouped[n][:],
                     op0=ALU.subtract,
                     op1=ALU.mult,
                 )
 
         def exponential(task):
-            centre = CENTRES[task % GROUPS]
+            g = task % GROUPS
+            left_out = 0.0 if g < SCALAR_SQUARES else CENTRES[g] * CENTRES[g]
             rbf[task] = rbfs.tile([P, BLOCK_COLS], BF16, align_bytes=64, name="rbf")
             nc.scalar.activation(
                 out=rbf[task][:],
                 in_=distance[task][:],
                 func=ACT.Exp,
                 scale=-SHARPNESS,
-                bias=-SHARPNESS * centre * centre,
+                bias=-SHARPNESS * left_out,
             )
 
         def product(task):
@@ -256,8 +239,6 @@ def tile_kandense_kernel(tc, x, base_weight_words, base_weight_scales, spline_we
 
         transpose_block(0)
         group_block(0)
-        for g in range(GROUPS):
-            regroup_weight(g)
         for step in range(TASKS + AHEAD + BEHIND + 1):
             n, g = divmod(step, GROUPS)
             if n + 1 < BLOCKS:
@@ -275,6 +256,8 @@ def tile_kandense_kernel(tc, x, base_weight_words, base_weight_scales, spline_we
                     silu_block(n)
             if 0 <= step - AHEAD < TASKS:
                 exponential(step - AHEAD)
+            if 0 <= step - AHEAD < GROUPS:
+                regroup_weight(step - AHEAD)
             ripe = step - AHEAD - BEHIND
             if ripe > 0 and ripe % GROUPS == 0:
                 finish_block(ripe // GROUPS - 1)

@@ -27,12 +27,12 @@ TILES = 2
 BLOCKS = ROWS // (TILES * P)
 TILE_COLS = PASSES * P * PACK
 BLOCK_COLS = TILES * TILE_COLS
-TASKS = BLOCKS * GROUPS
 
-SCALAR_SQUARES = 1
-
-AHEAD = 2
-BEHIND = 2
+ON_SCALAR = 0
+ON_GPSIMD = 2
+assert CENTRES[ON_GPSIMD] == 0.0
+ON_VECTOR = (1, 3, 4)
+ROUND_ORDER = (1, 2, 3, 4, 0)
 
 FLOPS = 2 * ROWS * FEATURES * UNITS * (1 + GROUPS)
 BYTES = (
@@ -53,11 +53,11 @@ def tile_kandense_kernel(tc, x, base_weight_words, base_weight_scales, spline_we
         keep = ctx.enter_context(tc.tile_pool(name="keep", bufs=1))
         x_pool = ctx.enter_context(tc.tile_pool(name="x_pool", bufs=BLOCKS))
         by_block = ctx.enter_context(tc.tile_pool(name="by_block", bufs=2))
-        distances = ctx.enter_context(tc.tile_pool(name="distances", bufs=AHEAD + 2))
-        rbfs = ctx.enter_context(tc.tile_pool(name="rbfs", bufs=BEHIND + 2))
+        distances = ctx.enter_context(tc.tile_pool(name="distances", bufs=2))
+        rbfs = ctx.enter_context(tc.tile_pool(name="rbfs", bufs=GROUPS + 2))
         coded = ctx.enter_context(tc.tile_pool(name="coded", bufs=4))
-        x_psum = ctx.enter_context(tc.psum_pool(name="x_psum", bufs=TILES))
-        sums = ctx.enter_context(tc.psum_pool(name="sums", bufs=2))
+        x_psum = ctx.enter_context(tc.psum_pool(name="x_psum", bufs=2 * TILES))
+        sums = ctx.enter_context(tc.psum_pool(name="sums", bufs=1))
         ctx.enter_context(tc.manual_schedule())
 
         x_rows = []
@@ -99,10 +99,9 @@ def tile_kandense_kernel(tc, x, base_weight_words, base_weight_scales, spline_we
         w_by_slice = w_rows[:].rearrange("p c t (u s) -> p s c u t", s=SLICES)
 
         def regroup_weight(g):
-            if g % 2 == 0:
-                nc.vector.tensor_copy(out=w_grouped[:, g], in_=w_by_slice[:, g])
-            else:
-                nc.scalar.copy(out=w_grouped[:, g], in_=w_by_slice[:, g])
+            nc.gpsimd.tensor_scalar(
+                out=w_grouped[:, g], in0=w_by_slice[:, g], scalar1=1.0, scalar2=0.0, op0=ALU.mult, op1=ALU.add
+            )
 
         def quantise_weight(g):
             nc.vector.quantize_mx(
@@ -154,12 +153,47 @@ def tile_kandense_kernel(tc, x, base_weight_words, base_weight_scales, spline_we
         def group_block(n):
             x_grouped[n] = by_block.tile([P, BLOCK_COLS], BF16, align_bytes=64, name="x_grouped")
             for j in range(TILES):
-                words_out = x_grouped[n][:, j * TILE_COLS : (j + 1) * TILE_COLS].bitcast(F32)
-                words_in = x_banks[n][j][:].rearrange("p c r u -> p (c r u)")
-                if j % 2 == 0:
-                    nc.vector.tensor_copy(out=words_out, in_=words_in)
-                else:
-                    nc.scalar.copy(out=words_out, in_=words_in)
+                nc.vector.tensor_copy(
+                    out=x_grouped[n][:, j * TILE_COLS : (j + 1) * TILE_COLS].bitcast(F32),
+                    in_=x_banks[n][j][:].rearrange("p c r u -> p (c r u)"),
+                )
+
+        def gpsimd_distance(n):
+            middle = distances.tile([P, BLOCK_COLS], F32)
+            for j in range(TILES):
+                cols = slice(j * TILE_COLS, (j + 1) * TILE_COLS)
+                nc.gpsimd.tensor_tensor(
+                    out=middle[:, cols], in0=x_grouped[n][:, cols], in1=x_grouped[n][:, cols], op=ALU.mult
+                )
+            distance[n, ON_GPSIMD] = middle
+
+        def vector_distance(n, g):
+            distance[n, g] = distances.tile([P, BLOCK_COLS], F32, name="distance%d" % g)
+            for j in range(TILES):
+                cols = slice(j * TILE_COLS, (j + 1) * TILE_COLS)
+                nc.vector.scalar_tensor_tensor(
+                    out=distance[n, g][:, cols],
+                    in0=x_banks[n][j][:].rearrange("p c r u -> p (c r u)").bitcast(BF16),
+                    scalar=2.0 * CENTRES[g],
+                    in1=x_grouped[n][:, cols],
+                    op0=ALU.subtract,
+                    op1=ALU.mult,
+                )
+
+        def scalar_distance(n):
+            whole = distances.tile([P, BLOCK_COLS], F32)
+            nc.scalar.activation(out=whole[:], in_=x_grouped[n][:], func=ACT.Square, bias=-CENTRES[ON_SCALAR])
+            distance[n, ON_SCALAR] = whole
+
+        def exponential(n, g, left_out):
+            rbf[n, g] = rbfs.tile([P, BLOCK_COLS], BF16, align_bytes=64, name="rbf")
+            nc.scalar.activation(
+                out=rbf[n, g][:],
+                in_=distance[n, g][:],
+                func=ACT.Exp,
+                scale=-SHARPNESS,
+                bias=-SHARPNESS * left_out,
+            )
 
         def base_product(n):
             x_codes, x_scales = quantise_block(x_grouped[n][:])
@@ -184,44 +218,14 @@ def tile_kandense_kernel(tc, x, base_weight_words, base_weight_scales, spline_we
                 op1=ALU.mult,
             )
 
-        def squared_distance(task):
-            n, g = divmod(task, GROUPS)
-            distance[task] = distances.tile([P, BLOCK_COLS], F32, name="distance")
-            if g < SCALAR_SQUARES:
-                nc.scalar.activation(
-                    out=distance[task][:], in_=x_grouped[n][:], func=ACT.Square, bias=-CENTRES[g]
-                )
-            else:
-                nc.vector.scalar_tensor_tensor(
-                    out=distance[task][:],
-                    in0=x_grouped[n][:],
-                    scalar=2.0 * CENTRES[g],
-                    in1=x_grouped[n][:],
-                    op0=ALU.subtract,
-                    op1=ALU.mult,
-                )
-
-        def exponential(task):
-            g = task % GROUPS
-            left_out = 0.0 if g < SCALAR_SQUARES else CENTRES[g] * CENTRES[g]
-            rbf[task] = rbfs.tile([P, BLOCK_COLS], BF16, align_bytes=64, name="rbf")
-            nc.scalar.activation(
-                out=rbf[task][:],
-                in_=distance[task][:],
-                func=ACT.Exp,
-                scale=-SHARPNESS,
-                bias=-SHARPNESS * left_out,
-            )
-
-        def product(task):
-            n, g = divmod(task, GROUPS)
-            if g == 0:
+        def product(n, g):
+            if g == ROUND_ORDER[0]:
                 spline_sum[n] = [sums.tile([P, UNITS], F32, name="spline_sum%d" % j) for j in range(TILES)]
-            rbf_codes, rbf_scales = quantise_block(rbf[task][:])
+            rbf_codes, rbf_scales = quantise_block(rbf[n, g][:])
             for j in range(TILES):
                 multiply(
                     spline_sum[n][j][:], rbf_codes, rbf_scales, j, w_codes[:, g], w_scales[:, g],
-                    g == 0, g == GROUPS - 1,
+                    g == ROUND_ORDER[0], g == ROUND_ORDER[-1],
                 )
 
         def finish_block(n):
@@ -238,30 +242,36 @@ def tile_kandense_kernel(tc, x, base_weight_words, base_weight_scales, spline_we
             nc.sync.dma_start(out=out_blocks[n], in_=result[:])
 
         transpose_block(0)
-        group_block(0)
-        for step in range(TASKS + AHEAD + BEHIND + 1):
-            n, g = divmod(step, GROUPS)
-            if n + 1 < BLOCKS:
-                if g == 1:
-                    transpose_block(n + 1)
-                if g == 2:
-                    group_block(n + 1)
-            if step < TASKS:
-                squared_distance(step)
-                if g == 0:
-                    base_product(n)
-                if g == 2:
-                    tanh_block(n)
-                if g == 3:
-                    silu_block(n)
-            if 0 <= step - AHEAD < TASKS:
-                exponential(step - AHEAD)
-            if 0 <= step - AHEAD < GROUPS:
-                regroup_weight(step - AHEAD)
-            ripe = step - AHEAD - BEHIND
-            if ripe > 0 and ripe % GROUPS == 0:
-                finish_block(ripe // GROUPS - 1)
-            if 0 <= ripe < GROUPS:
-                quantise_weight(ripe)
-            if 0 <= ripe < TASKS:
-                product(ripe)
+        for k in range(-1, BLOCKS):
+            if k + 1 < BLOCKS:
+                group_block(k + 1)
+                gpsimd_distance(k + 1)
+            if k == -1:
+                for g in range(GROUPS):
+                    regroup_weight(g)
+            if k >= 1:
+                finish_block(k - 1)
+            if k + 1 < BLOCKS:
+                for g in ON_VECTOR:
+                    vector_distance(k + 1, g)
+            if k == BLOCKS - 1:
+                vector_distance(k, ON_SCALAR)
+            if 0 <= k < BLOCKS - 1:
+                scalar_distance(k)
+            if k >= 0:
+                for g in ROUND_ORDER:
+                    by_square = g == ON_SCALAR and k < BLOCKS - 1
+                    exponential(k, g, 0.0 if by_square else CENTRES[g] * CENTRES[g])
+                    if g == 3:
+                        tanh_block(k)
+                silu_block(k)
+            if k + 2 < BLOCKS:
+                transpose_block(k + 2)
+            if k + 1 < BLOCKS:
+                base_product(k + 1)
+            if k >= 0:
+                for g in ROUND_ORDER:
+                    if k == 0:
+                        quantise_weight(g)
+                    product(k, g)
+        finish_block(BLOCKS - 1)

@@ -33,6 +33,8 @@ ON_GPSIMD = 2
 assert CENTRES[ON_GPSIMD] == 0.0
 ON_VECTOR = (1, 3, 4)
 ROUND_ORDER = (1, 2, 3, 4, 0)
+REGROUP_IN_ROUND = {-1: ROUND_ORDER[:1], 0: ROUND_ORDER[1:3], 1: ROUND_ORDER[3:]}
+WEIGHTS_ROUND = 2
 
 FLOPS = 2 * ROWS * FEATURES * UNITS * (1 + GROUPS)
 BYTES = (
@@ -55,9 +57,12 @@ def tile_kandense_kernel(tc, x, base_weight_words, base_weight_scales, spline_we
         by_block = ctx.enter_context(tc.tile_pool(name="by_block", bufs=2))
         distances = ctx.enter_context(tc.tile_pool(name="distances", bufs=2))
         rbfs = ctx.enter_context(tc.tile_pool(name="rbfs", bufs=GROUPS + 2))
-        coded = ctx.enter_context(tc.tile_pool(name="coded", bufs=4))
+        coded = ctx.enter_context(tc.tile_pool(name="coded", bufs=2))
+        waiting = ctx.enter_context(tc.tile_pool(name="waiting", bufs=WEIGHTS_ROUND * GROUPS + 2))
+        silus = ctx.enter_context(tc.tile_pool(name="silus", bufs=WEIGHTS_ROUND + 1))
         x_psum = ctx.enter_context(tc.psum_pool(name="x_psum", bufs=2 * TILES))
         sums = ctx.enter_context(tc.psum_pool(name="sums", bufs=1))
+        spline_sums = ctx.enter_context(tc.psum_pool(name="spline_sums", bufs=WEIGHTS_ROUND + 1))
         ctx.enter_context(tc.manual_schedule())
 
         x_rows = []
@@ -80,14 +85,12 @@ def tile_kandense_kernel(tc, x, base_weight_words, base_weight_scales, spline_we
                 in_=scale_rows[4 * quadrant : 4 * quadrant + 4].bitcast(I32),
             )
 
-        nc.sync.dma_start(out=x_rows[1][:], in_=x_blocks[1])
-
         w_rows = keep.tile([P, PASSES, PACK, UNITS * SLICES], BF16)
         nc.sync.dma_start(
             out=w_rows[:],
             in_=spline_weight.rearrange("(c p t) u s -> p c t (u s)", p=P, t=PACK),
         )
-        for n in range(2, BLOCKS):
+        for n in range(1, BLOCKS):
             nc.sync.dma_start(out=x_rows[n][:], in_=x_blocks[n])
 
         identity = keep.tile([P, P], F32)
@@ -110,9 +113,9 @@ def tile_kandense_kernel(tc, x, base_weight_words, base_weight_scales, spline_we
                 in_=w_grouped[:, g].rearrange("p c u t -> p (c u t)"),
             )
 
-        def quantise_block(values):
-            codes = coded.tile([P, TILES, PASSES, P], U32, align_bytes=64, name="codes")
-            scales = coded.tile([P, TILES, PASSES, P], U8, align_bytes=64, name="scales")
+        def quantise_block(values, pool):
+            codes = pool.tile([P, TILES, PASSES, P], U32, align_bytes=64, name="codes")
+            scales = pool.tile([P, TILES, PASSES, P], U8, align_bytes=64, name="scales")
             nc.vector.quantize_mx(
                 out=codes[:].rearrange("p j c r -> p (j c r)").bitcast(FP8X4),
                 scales=scales[:].rearrange("p j c r -> p (j c r)"),
@@ -133,7 +136,7 @@ def tile_kandense_kernel(tc, x, base_weight_words, base_weight_scales, spline_we
                 )
 
         x_banks, x_grouped, base_sum, tanh_half, twice_silu, spline_sum = {}, {}, {}, {}, {}, {}
-        distance, rbf = {}, {}
+        distance, rbf, rbf_coded = {}, {}, {}
 
         def transpose_block(n):
             x_words = x_rows[n][:].bitcast(F32)
@@ -181,7 +184,7 @@ def tile_kandense_kernel(tc, x, base_weight_words, base_weight_scales, spline_we
                 )
 
         def scalar_distance(n):
-            whole = distances.tile([P, BLOCK_COLS], F32)
+            whole = distances.tile([P, BLOCK_COLS], F32, name="distance%d" % ON_SCALAR)
             nc.scalar.activation(out=whole[:], in_=x_grouped[n][:], func=ACT.Square, bias=-CENTRES[ON_SCALAR])
             distance[n, ON_SCALAR] = whole
 
@@ -196,7 +199,7 @@ def tile_kandense_kernel(tc, x, base_weight_words, base_weight_scales, spline_we
             )
 
         def base_product(n):
-            x_codes, x_scales = quantise_block(x_grouped[n][:])
+            x_codes, x_scales = quantise_block(x_grouped[n][:], coded)
             base_sum[n] = sums.tile([P, TILES, UNITS], F32, name="base_sum")
             for j in range(TILES):
                 multiply(base_sum[n][:, j, :], x_codes, x_scales, j, base_codes, base_scales, True, True)
@@ -208,7 +211,7 @@ def tile_kandense_kernel(tc, x, base_weight_words, base_weight_scales, spline_we
             )
 
         def silu_block(n):
-            twice_silu[n] = by_block.tile([P, TILES, UNITS], F32, name="twice_silu")
+            twice_silu[n] = silus.tile([P, TILES, UNITS], F32, name="twice_silu")
             nc.vector.scalar_tensor_tensor(
                 out=twice_silu[n][:].rearrange("p j u -> p (j u)"),
                 in0=tanh_half[n][:],
@@ -218,44 +221,63 @@ def tile_kandense_kernel(tc, x, base_weight_words, base_weight_scales, spline_we
                 op1=ALU.mult,
             )
 
-        def product(n, g):
-            if g == ROUND_ORDER[0]:
-                spline_sum[n] = [sums.tile([P, UNITS], F32, name="spline_sum%d" % j) for j in range(TILES)]
-            rbf_codes, rbf_scales = quantise_block(rbf[n, g][:])
+        def quantise_rbf(n, g):
+            rbf_coded[n, g] = quantise_block(rbf[n, g][:], waiting)
+
+        def open_sums(n):
+            if n == BLOCKS - 1:
+                spline_sum[n] = [spline_sums.tile([P, UNITS], F32, name="spline_sum") for j in range(TILES)]
+            else:
+                spline_sum[n] = [spline_sums.tile([P, TILES, UNITS], F32, name="spline_sum")]
+
+        def product(n, g, j):
+            acc = spline_sum[n][j][:] if n == BLOCKS - 1 else spline_sum[n][0][:, j, :]
+            rbf_codes, rbf_scales = rbf_coded[n, g]
+            multiply(
+                acc, rbf_codes, rbf_scales, j, w_codes[:, g], w_scales[:, g],
+                g == ROUND_ORDER[0], g == ROUND_ORDER[-1],
+            )
+
+        def products(n):
+            open_sums(n)
             for j in range(TILES):
-                multiply(
-                    spline_sum[n][j][:], rbf_codes, rbf_scales, j, w_codes[:, g], w_scales[:, g],
-                    g == ROUND_ORDER[0], g == ROUND_ORDER[-1],
-                )
+                for g in ROUND_ORDER:
+                    product(n, g, j)
 
         def finish_block(n):
             result = by_block.tile([P, TILES, UNITS], F32)
-            for j in range(TILES):
+            if n == BLOCKS - 1:
+                pieces = [(result[:, j, :], twice_silu[n][:, j, :], spline_sum[n][j][:]) for j in range(TILES)]
+            else:
+                pieces = [
+                    (
+                        result[:].rearrange("p j u -> p (j u)"),
+                        twice_silu[n][:].rearrange("p j u -> p (j u)"),
+                        spline_sum[n][0][:].rearrange("p j u -> p (j u)"),
+                    )
+                ]
+            for whole, silu_part, spline_part in pieces:
                 nc.vector.scalar_tensor_tensor(
-                    out=result[:, j, :],
-                    in0=twice_silu[n][:, j, :],
-                    scalar=0.5,
-                    in1=spline_sum[n][j][:],
-                    op0=ALU.mult,
-                    op1=ALU.add,
+                    out=whole, in0=silu_part, scalar=0.5, in1=spline_part, op0=ALU.mult, op1=ALU.add
                 )
             nc.sync.dma_start(out=out_blocks[n], in_=result[:])
 
         transpose_block(0)
+        multiplied = []
         for k in range(-1, BLOCKS):
             if k + 1 < BLOCKS:
                 group_block(k + 1)
                 gpsimd_distance(k + 1)
-            if k == -1:
-                for g in range(GROUPS):
-                    regroup_weight(g)
-            if k >= 1:
-                finish_block(k - 1)
+            for g in REGROUP_IN_ROUND.get(k, ()):
+                regroup_weight(g)
             if k + 1 < BLOCKS:
                 for g in ON_VECTOR:
                     vector_distance(k + 1, g)
             if k == BLOCKS - 1:
                 vector_distance(k, ON_SCALAR)
+            for n in multiplied:
+                finish_block(n)
+            multiplied.clear()
             if 0 <= k < BLOCKS - 1:
                 scalar_distance(k)
             if k >= 0:
@@ -269,9 +291,22 @@ def tile_kandense_kernel(tc, x, base_weight_words, base_weight_scales, spline_we
                 transpose_block(k + 2)
             if k + 1 < BLOCKS:
                 base_product(k + 1)
-            if k >= 0:
+            if k == WEIGHTS_ROUND:
                 for g in ROUND_ORDER:
-                    if k == 0:
-                        quantise_weight(g)
-                    product(k, g)
+                    quantise_weight(g)
+                for n in range(WEIGHTS_ROUND):
+                    products(n)
+                    multiplied.append(n)
+            if k == BLOCKS - 1:
+                open_sums(k)
+                for g in ROUND_ORDER:
+                    quantise_rbf(k, g)
+                    for j in range(TILES):
+                        product(k, g, j)
+            elif k >= 0:
+                for g in ROUND_ORDER:
+                    quantise_rbf(k, g)
+                if k >= WEIGHTS_ROUND:
+                    products(k)
+                    multiplied.append(k)
         finish_block(BLOCKS - 1)

@@ -36,6 +36,11 @@ ROUND_ORDER = (1, 2, 3, 4, 0)
 REGROUP_IN_ROUND = {-1: ROUND_ORDER[:1], 0: ROUND_ORDER[1:3], 1: ROUND_ORDER[3:]}
 WEIGHTS_ROUND = 2
 
+
+def round_order(n):
+    return ROUND_ORDER[-1:] + ROUND_ORDER[:-1] if n == 0 else ROUND_ORDER
+
+
 FLOPS = 2 * ROWS * FEATURES * UNITS * (1 + GROUPS)
 BYTES = (
     2 * ROWS * FEATURES
@@ -68,7 +73,10 @@ def tile_kandense_kernel(tc, x, base_weight_words, base_weight_scales, spline_we
         x_rows = []
         for n in range(BLOCKS):
             x_rows.append(x_pool.tile([P, TILES, FEATURES], BF16, name="x_rows"))
-        nc.sync.dma_start(out=x_rows[0][:], in_=x_blocks[0])
+        for c in range(PASSES):
+            for j in range(TILES):
+                ks = slice(c * K_PASS, (c + 1) * K_PASS)
+                nc.sync.dma_start(out=x_rows[0][:, j, ks], in_=x_blocks[0][:, j, ks])
 
         base_codes = keep.tile([P, PASSES, UNITS], U32, align_bytes=64)
         for c in range(PASSES):
@@ -113,14 +121,16 @@ def tile_kandense_kernel(tc, x, base_weight_words, base_weight_scales, spline_we
                 in_=w_grouped[:, g].rearrange("p c u t -> p (c u t)"),
             )
 
-        def quantise_block(values, pool):
+        def quantise_block(values, pool, groups_of_tiles=1):
             codes = pool.tile([P, TILES, PASSES, P], U32, align_bytes=64, name="codes")
             scales = pool.tile([P, TILES, PASSES, P], U8, align_bytes=64, name="scales")
-            nc.vector.quantize_mx(
-                out=codes[:].rearrange("p j c r -> p (j c r)").bitcast(FP8X4),
-                scales=scales[:].rearrange("p j c r -> p (j c r)"),
-                in_=values,
-            )
+            step = TILES // groups_of_tiles
+            for j in range(0, TILES, step):
+                nc.vector.quantize_mx(
+                    out=codes[:, j : j + step].rearrange("p j c r -> p (j c r)").bitcast(FP8X4),
+                    scales=scales[:, j : j + step].rearrange("p j c r -> p (j c r)"),
+                    in_=values[:, j * TILE_COLS : (j + step) * TILE_COLS],
+                )
             return codes, scales
 
         def multiply(acc, codes, scales, j, weight_codes, weight_scales, first, last):
@@ -138,28 +148,40 @@ def tile_kandense_kernel(tc, x, base_weight_words, base_weight_scales, spline_we
         x_banks, x_grouped, base_sum, tanh_half, twice_silu, spline_sum = {}, {}, {}, {}, {}, {}
         distance, rbf, rbf_coded = {}, {}, {}
 
+        def transpose_piece(n, j, c):
+            first_word = c * K_PASS // 2
+            for u in range(PAIRS):
+                nc.tensor.transpose(
+                    x_banks[n][j][:, c, :, u],
+                    x_rows[n][:].bitcast(F32)[:, j, first_word + u : first_word + K_PASS // 2 : PAIRS],
+                    identity[:],
+                )
+
+        def new_banks(n):
+            x_banks[n] = [x_psum.tile([P, PASSES, P, PAIRS], F32, name="x_bank") for j in range(TILES)]
+
         def transpose_block(n):
-            x_words = x_rows[n][:].bitcast(F32)
-            x_banks[n] = []
+            new_banks(n)
             for j in range(TILES):
-                x_bank = x_psum.tile([P, PASSES, P, PAIRS], F32)
                 for c in range(PASSES):
-                    first_word = c * K_PASS // 2
-                    for u in range(PAIRS):
-                        nc.tensor.transpose(
-                            x_bank[:, c, :, u],
-                            x_words[:, j, first_word + u : first_word + K_PASS // 2 : PAIRS],
-                            identity[:],
-                        )
-                x_banks[n].append(x_bank)
+                    transpose_piece(n, j, c)
+
+        def group_piece(n, j, passes):
+            nc.vector.tensor_copy(
+                out=x_grouped[n][:, piece_cols(j, passes)].bitcast(F32),
+                in_=x_banks[n][j][:, passes, :, :].rearrange("p c r u -> p (c r u)"),
+            )
+
+        def piece_cols(j, passes):
+            return slice(j * TILE_COLS + passes.start * P * PACK, j * TILE_COLS + passes.stop * P * PACK)
+
+        def new_grouped(n):
+            x_grouped[n] = by_block.tile([P, BLOCK_COLS], BF16, align_bytes=64, name="x_grouped")
 
         def group_block(n):
-            x_grouped[n] = by_block.tile([P, BLOCK_COLS], BF16, align_bytes=64, name="x_grouped")
+            new_grouped(n)
             for j in range(TILES):
-                nc.vector.tensor_copy(
-                    out=x_grouped[n][:, j * TILE_COLS : (j + 1) * TILE_COLS].bitcast(F32),
-                    in_=x_banks[n][j][:].rearrange("p c r u -> p (c r u)"),
-                )
+                group_piece(n, j, slice(0, PASSES))
 
         def gpsimd_distance(n):
             middle = distances.tile([P, BLOCK_COLS], F32)
@@ -183,20 +205,24 @@ def tile_kandense_kernel(tc, x, base_weight_words, base_weight_scales, spline_we
                     op1=ALU.mult,
                 )
 
-        def scalar_distance(n):
-            whole = distances.tile([P, BLOCK_COLS], F32, name="distance%d" % ON_SCALAR)
-            nc.scalar.activation(out=whole[:], in_=x_grouped[n][:], func=ACT.Square, bias=-CENTRES[ON_SCALAR])
-            distance[n, ON_SCALAR] = whole
-
-        def exponential(n, g, left_out):
-            rbf[n, g] = rbfs.tile([P, BLOCK_COLS], BF16, align_bytes=64, name="rbf")
+        def scalar_distance(n, cols):
+            if cols.start == 0:
+                distance[n, ON_SCALAR] = distances.tile([P, BLOCK_COLS], F32, name="distance%d" % ON_SCALAR)
             nc.scalar.activation(
-                out=rbf[n, g][:],
-                in_=distance[n, g][:],
-                func=ACT.Exp,
-                scale=-SHARPNESS,
-                bias=-SHARPNESS * left_out,
+                out=distance[n, ON_SCALAR][:, cols], in_=x_grouped[n][:, cols], func=ACT.Square, bias=-CENTRES[ON_SCALAR]
             )
+
+        def exponential(n, g, left_out, pieces=1):
+            rbf[n, g] = rbfs.tile([P, BLOCK_COLS], BF16, align_bytes=64, name="rbf")
+            width = BLOCK_COLS // pieces
+            for first_col in range(0, BLOCK_COLS, width):
+                nc.scalar.activation(
+                    out=rbf[n, g][:, first_col : first_col + width],
+                    in_=distance[n, g][:, first_col : first_col + width],
+                    func=ACT.Exp,
+                    scale=-SHARPNESS,
+                    bias=-SHARPNESS * left_out,
+                )
 
         def base_product(n):
             x_codes, x_scales = quantise_block(x_grouped[n][:], coded)
@@ -221,8 +247,8 @@ def tile_kandense_kernel(tc, x, base_weight_words, base_weight_scales, spline_we
                 op1=ALU.mult,
             )
 
-        def quantise_rbf(n, g):
-            rbf_coded[n, g] = quantise_block(rbf[n, g][:], waiting)
+        def quantise_rbf(n, g, groups_of_tiles=1):
+            rbf_coded[n, g] = quantise_block(rbf[n, g][:], waiting, groups_of_tiles)
 
         def open_sums(n):
             if n == BLOCKS - 1:
@@ -247,26 +273,37 @@ def tile_kandense_kernel(tc, x, base_weight_words, base_weight_scales, spline_we
         def finish_block(n):
             result = by_block.tile([P, TILES, UNITS], F32)
             if n == BLOCKS - 1:
-                pieces = [(result[:, j, :], twice_silu[n][:, j, :], spline_sum[n][j][:]) for j in range(TILES)]
-            else:
-                pieces = [
-                    (
-                        result[:].rearrange("p j u -> p (j u)"),
-                        twice_silu[n][:].rearrange("p j u -> p (j u)"),
-                        spline_sum[n][0][:].rearrange("p j u -> p (j u)"),
+                for j in range(TILES):
+                    nc.vector.scalar_tensor_tensor(
+                        out=result[:, j, :], in0=twice_silu[n][:, j, :], scalar=0.5, in1=spline_sum[n][j][:],
+                        op0=ALU.mult, op1=ALU.add,
                     )
-                ]
-            for whole, silu_part, spline_part in pieces:
+                    nc.sync.dma_start(out=out_blocks[n][:, j, :], in_=result[:, j, :])
+            else:
                 nc.vector.scalar_tensor_tensor(
-                    out=whole, in0=silu_part, scalar=0.5, in1=spline_part, op0=ALU.mult, op1=ALU.add
+                    out=result[:].rearrange("p j u -> p (j u)"),
+                    in0=twice_silu[n][:].rearrange("p j u -> p (j u)"),
+                    scalar=0.5,
+                    in1=spline_sum[n][0][:].rearrange("p j u -> p (j u)"),
+                    op0=ALU.mult,
+                    op1=ALU.add,
                 )
-            nc.sync.dma_start(out=out_blocks[n], in_=result[:])
+                nc.sync.dma_start(out=out_blocks[n], in_=result[:])
 
-        transpose_block(0)
+        new_banks(0)
+        new_grouped(0)
+        for c in range(PASSES):
+            for j in range(TILES):
+                transpose_piece(0, j, c)
+                group_piece(0, j, slice(c, c + 1))
+        for c in range(PASSES):
+            for j in range(TILES):
+                scalar_distance(0, piece_cols(j, slice(c, c + 1)))
         multiplied = []
         for k in range(-1, BLOCKS):
             if k + 1 < BLOCKS:
-                group_block(k + 1)
+                if k + 1 > 0:
+                    group_block(k + 1)
                 gpsimd_distance(k + 1)
             for g in REGROUP_IN_ROUND.get(k, ()):
                 regroup_weight(g)
@@ -278,12 +315,13 @@ def tile_kandense_kernel(tc, x, base_weight_words, base_weight_scales, spline_we
             for n in multiplied:
                 finish_block(n)
             multiplied.clear()
-            if 0 <= k < BLOCKS - 1:
-                scalar_distance(k)
+            if 0 < k < BLOCKS - 1:
+                scalar_distance(k, slice(0, BLOCK_COLS))
             if k >= 0:
-                for g in ROUND_ORDER:
+                for g in round_order(k):
                     by_square = g == ON_SCALAR and k < BLOCKS - 1
-                    exponential(k, g, 0.0 if by_square else CENTRES[g] * CENTRES[g])
+                    pieces = TILES if (k == BLOCKS - 1 and g == ROUND_ORDER[-1]) else 1
+                    exponential(k, g, 0.0 if by_square else CENTRES[g] * CENTRES[g], pieces)
                     if g == 3:
                         tanh_block(k)
                 silu_block(k)
@@ -300,11 +338,11 @@ def tile_kandense_kernel(tc, x, base_weight_words, base_weight_scales, spline_we
             if k == BLOCKS - 1:
                 open_sums(k)
                 for g in ROUND_ORDER:
-                    quantise_rbf(k, g)
+                    quantise_rbf(k, g, TILES if g == ROUND_ORDER[-1] else 1)
                     for j in range(TILES):
                         product(k, g, j)
             elif k >= 0:
-                for g in ROUND_ORDER:
+                for g in round_order(k):
                     quantise_rbf(k, g)
                 if k >= WEIGHTS_ROUND:
                     products(k)

@@ -35,6 +35,11 @@ ON_VECTOR = (1, 3, 4)
 ROUND_ORDER = (1, 2, 3, 4, 0)
 REGROUP_IN_ROUND = {-1: ROUND_ORDER[:1], 0: ROUND_ORDER[1:3], 1: ROUND_ORDER[3:]}
 WEIGHTS_ROUND = 2
+SHARED = 3
+assert CENTRES[SHARED] == 0.5
+SHARED_BLOCKS = (WEIGHTS_ROUND + 1, WEIGHTS_ROUND + 2)
+JUST_IN_TIME = ((BLOCKS - 1, ROUND_ORDER[-2]), (BLOCKS - 1, ON_SCALAR))
+SCALAR_BLOCKS = range(BLOCKS - 2)
 
 
 def round_order(n):
@@ -191,10 +196,18 @@ def tile_kandense_kernel(tc, x, base_weight_words, base_weight_scales, spline_we
                     out=middle[:, cols], in0=x_grouped[n][:, cols], in1=x_grouped[n][:, cols], op=ALU.mult
                 )
             distance[n, ON_GPSIMD] = middle
+            if n in SHARED_BLOCKS:
+                distance[n, SHARED] = distances.tile([P, BLOCK_COLS], F32, name="distance%d" % SHARED)
+                first = slice(0, TILE_COLS)
+                nc.gpsimd.tensor_tensor(
+                    out=distance[n, SHARED][:, first], in0=middle[:, first], in1=x_grouped[n][:, first], op=ALU.subtract
+                )
 
         def vector_distance(n, g):
-            distance[n, g] = distances.tile([P, BLOCK_COLS], F32, name="distance%d" % g)
-            for j in range(TILES):
+            shared = g == SHARED and n in SHARED_BLOCKS
+            if not shared:
+                distance[n, g] = distances.tile([P, BLOCK_COLS], F32, name="distance%d" % g)
+            for j in range(1 if shared else 0, TILES):
                 cols = slice(j * TILE_COLS, (j + 1) * TILE_COLS)
                 nc.vector.scalar_tensor_tensor(
                     out=distance[n, g][:, cols],
@@ -299,8 +312,26 @@ def tile_kandense_kernel(tc, x, base_weight_words, base_weight_scales, spline_we
         for c in range(PASSES):
             for j in range(TILES):
                 scalar_distance(0, piece_cols(j, slice(c, c + 1)))
+        complete = []
         multiplied = []
+
+        def last_quantise(n):
+            quantise_rbf(n, round_order(n)[-1])
+            complete.append(n)
+
+        def multiply_complete_blocks():
+            for n in complete:
+                products(n)
+                multiplied.append(n)
+            complete.clear()
+
         for k in range(-1, BLOCKS):
+            if k == BLOCKS - 1:
+                last_quantise(k - 1)
+                multiply_complete_blocks()
+            for n, g in JUST_IN_TIME:
+                if n == k:
+                    vector_distance(n, g)
             if k + 1 < BLOCKS:
                 if k + 1 > 0:
                     group_block(k + 1)
@@ -308,18 +339,17 @@ def tile_kandense_kernel(tc, x, base_weight_words, base_weight_scales, spline_we
             for g in REGROUP_IN_ROUND.get(k, ()):
                 regroup_weight(g)
             if k + 1 < BLOCKS:
-                for g in ON_VECTOR:
-                    vector_distance(k + 1, g)
-            if k == BLOCKS - 1:
-                vector_distance(k, ON_SCALAR)
+                for g in ON_VECTOR + (() if k + 1 in SCALAR_BLOCKS else (ON_SCALAR,)):
+                    if (k + 1, g) not in JUST_IN_TIME:
+                        vector_distance(k + 1, g)
             for n in multiplied:
                 finish_block(n)
             multiplied.clear()
-            if 0 < k < BLOCKS - 1:
+            if k > 0 and k in SCALAR_BLOCKS:
                 scalar_distance(k, slice(0, BLOCK_COLS))
             if k >= 0:
                 for g in round_order(k):
-                    by_square = g == ON_SCALAR and k < BLOCKS - 1
+                    by_square = g == ON_SCALAR and k in SCALAR_BLOCKS
                     pieces = TILES if (k == BLOCKS - 1 and g == ROUND_ORDER[-1]) else 1
                     exponential(k, g, 0.0 if by_square else CENTRES[g] * CENTRES[g], pieces)
                     if g == 3:
@@ -327,14 +357,15 @@ def tile_kandense_kernel(tc, x, base_weight_words, base_weight_scales, spline_we
                 silu_block(k)
             if k + 2 < BLOCKS:
                 transpose_block(k + 2)
+            if 1 <= k < BLOCKS - 1:
+                last_quantise(k - 1)
             if k + 1 < BLOCKS:
                 base_product(k + 1)
             if k == WEIGHTS_ROUND:
                 for g in ROUND_ORDER:
                     quantise_weight(g)
-                for n in range(WEIGHTS_ROUND):
-                    products(n)
-                    multiplied.append(n)
+            if WEIGHTS_ROUND <= k < BLOCKS - 1:
+                multiply_complete_blocks()
             if k == BLOCKS - 1:
                 open_sums(k)
                 for g in ROUND_ORDER:
@@ -342,9 +373,6 @@ def tile_kandense_kernel(tc, x, base_weight_words, base_weight_scales, spline_we
                     for j in range(TILES):
                         product(k, g, j)
             elif k >= 0:
-                for g in round_order(k):
+                for g in round_order(k)[:-1]:
                     quantise_rbf(k, g)
-                if k >= WEIGHTS_ROUND:
-                    products(k)
-                    multiplied.append(k)
         finish_block(BLOCKS - 1)

@@ -33,12 +33,12 @@ ON_GPSIMD = 2
 assert CENTRES[ON_GPSIMD] == 0.0
 ON_VECTOR = (1, 3, 4)
 ROUND_ORDER = (1, 2, 3, 4, 0)
-REGROUP_IN_ROUND = {-1: ROUND_ORDER[:1], 0: ROUND_ORDER[1:3], 1: ROUND_ORDER[3:]}
-WEIGHTS_ROUND = 2
+REGROUP_IN_ROUND = {-1: ROUND_ORDER[:1], 0: ROUND_ORDER[1:2], 1: ROUND_ORDER[2:3], 2: ROUND_ORDER[3:4], 3: ROUND_ORDER[4:]}
+WEIGHTS_ROUND = 3
 SHARED = 3
 assert CENTRES[SHARED] == 0.5
-SHARED_BLOCKS = (WEIGHTS_ROUND + 1, WEIGHTS_ROUND + 2)
-JUST_IN_TIME = ((BLOCKS - 1, ROUND_ORDER[-2]), (BLOCKS - 1, ON_SCALAR))
+SHARED_BLOCKS = (WEIGHTS_ROUND + 2,)
+JUST_IN_TIME = ((BLOCKS - 2, ON_SCALAR), (BLOCKS - 1, ROUND_ORDER[-2]), (BLOCKS - 1, ON_SCALAR))
 SCALAR_BLOCKS = range(BLOCKS - 2)
 
 
@@ -72,7 +72,7 @@ def tile_kandense_kernel(tc, x, base_weight_words, base_weight_scales, spline_we
         silus = ctx.enter_context(tc.tile_pool(name="silus", bufs=WEIGHTS_ROUND + 1))
         x_psum = ctx.enter_context(tc.psum_pool(name="x_psum", bufs=2 * TILES))
         sums = ctx.enter_context(tc.psum_pool(name="sums", bufs=1))
-        spline_sums = ctx.enter_context(tc.psum_pool(name="spline_sums", bufs=WEIGHTS_ROUND + 1))
+        spline_sums = ctx.enter_context(tc.psum_pool(name="spline_sums", bufs=WEIGHTS_ROUND))
         ctx.enter_context(tc.manual_schedule())
 
         x_rows = []
@@ -329,13 +329,13 @@ def tile_kandense_kernel(tc, x, base_weight_words, base_weight_scales, spline_we
             if k == BLOCKS - 1:
                 last_quantise(k - 1)
                 multiply_complete_blocks()
-            for n, g in JUST_IN_TIME:
-                if n == k:
-                    vector_distance(n, g)
             if k + 1 < BLOCKS:
                 if k + 1 > 0:
                     group_block(k + 1)
                 gpsimd_distance(k + 1)
+            for n, g in JUST_IN_TIME:
+                if n == k:
+                    vector_distance(n, g)
             for g in REGROUP_IN_ROUND.get(k, ()):
                 regroup_weight(g)
             if k + 1 < BLOCKS:
@@ -352,7 +352,7 @@ def tile_kandense_kernel(tc, x, base_weight_words, base_weight_scales, spline_we
                     by_square = g == ON_SCALAR and k in SCALAR_BLOCKS
                     pieces = TILES if (k == BLOCKS - 1 and g == ROUND_ORDER[-1]) else 1
                     exponential(k, g, 0.0 if by_square else CENTRES[g] * CENTRES[g], pieces)
-                    if g == 3:
+                    if g == (3 if k == 0 else round_order(k)[0]):
                         tanh_block(k)
                 silu_block(k)
             if k + 2 < BLOCKS:

from contextlib import ExitStack

import concourse.mybir as mybir
from concourse.masks import make_identity

F32 = mybir.dt.float32
BF16 = mybir.dt.bfloat16
I32 = mybir.dt.int32
U32 = mybir.dt.uint32
U8 = mybir.dt.uint8
FP8X4 = mybir.dt.float8_e4m3fn_x4
ACT = mybir.ActivationFunctionType
ALU = mybir.AluOpType

ROWS, FEATURES, UNITS, SLICES = 1536, 1024, 128, 8
CENTRES = (-1.0, -0.5, 0.0, 0.5, 1.0)
GROUPS = len(CENTRES)
SHARPNESS = 5.0

P = 128
PACK = 4
K_PASS = P * PACK
PASSES = FEATURES // K_PASS
PAIRS = PACK // 2

TILES = 2
BLOCKS = ROWS // (TILES * P)
TILE_COLS = PASSES * P * PACK
BLOCK_COLS = TILES * TILE_COLS

ON_SCALAR = 0
ON_GPSIMD = 2
assert CENTRES[ON_GPSIMD] == 0.0
ON_VECTOR = (1, 3, 4)
ROUND_ORDER = (1, 2, 3, 4, 0)
REGROUP_IN_ROUND = {-1: ROUND_ORDER[:1], 0: ROUND_ORDER[1:2], 1: ROUND_ORDER[2:3], 2: ROUND_ORDER[3:4], 3: ROUND_ORDER[4:]}
WEIGHTS_ROUND = 3
SHARED = 3
assert CENTRES[SHARED] == 0.5
SHARED_BLOCKS = (WEIGHTS_ROUND + 2,)
JUST_IN_TIME = ((BLOCKS - 2, ON_SCALAR), (BLOCKS - 1, ROUND_ORDER[-2]), (BLOCKS - 1, ON_SCALAR))
SCALAR_BLOCKS = range(BLOCKS - 2)


def round_order(n):
    return ROUND_ORDER[-1:] + ROUND_ORDER[:-1] if n == 0 else ROUND_ORDER


FLOPS = 2 * ROWS * FEATURES * UNITS * (1 + GROUPS)
BYTES = (
    2 * ROWS * FEATURES
    + FEATURES * UNITS
    + FEATURES // 32 * UNITS
    + 2 * FEATURES * UNITS * GROUPS
    + 4 * ROWS * UNITS
)


def tile_kandense_kernel(tc, x, base_weight_words, base_weight_scales, spline_weight, out):
    nc = tc.nc
    x_blocks = x.rearrange("(n p j) k -> n p j k", p=P, j=TILES)
    out_blocks = out.rearrange("(n p j) u -> n p j u", p=P, j=TILES)

    with ExitStack() as ctx:
        keep = ctx.enter_context(tc.tile_pool(name="keep", bufs=1))
        x_pool = ctx.enter_context(tc.tile_pool(name="x_pool", bufs=BLOCKS))
        by_block = ctx.enter_context(tc.tile_pool(name="by_block", bufs=2))
        distances = ctx.enter_context(tc.tile_pool(name="distances", bufs=2))
        rbfs = ctx.enter_context(tc.tile_pool(name="rbfs", bufs=GROUPS + 2))
        coded = ctx.enter_context(tc.tile_pool(name="coded", bufs=2))
        waiting = ctx.enter_context(tc.tile_pool(name="waiting", bufs=WEIGHTS_ROUND * GROUPS + 2))
        silus = ctx.enter_context(tc.tile_pool(name="silus", bufs=WEIGHTS_ROUND + 1))
        x_psum = ctx.enter_context(tc.psum_pool(name="x_psum", bufs=2 * TILES))
        sums = ctx.enter_context(tc.psum_pool(name="sums", bufs=1))
        spline_sums = ctx.enter_context(tc.psum_pool(name="spline_sums", bufs=WEIGHTS_ROUND))
        ctx.enter_context(tc.manual_schedule())

        x_rows = []
        for n in range(BLOCKS):
            x_rows.append(x_pool.tile([P, TILES, FEATURES], BF16, name="x_rows"))
        for c in range(PASSES):
            for j in range(TILES):
                ks = slice(c * K_PASS, (c + 1) * K_PASS)
                nc.sync.dma_start(out=x_rows[0][:, j, ks], in_=x_blocks[0][:, j, ks])

        base_codes = keep.tile([P, PASSES, UNITS], U32, align_bytes=64)
        for c in range(PASSES):
            nc.sync.dma_start(
                out=base_codes[:, c, :].bitcast(I32),
                in_=base_weight_words[c].rearrange("p n t -> p (n t)").bitcast(I32),
            )
        base_scales = keep.tile([P, PASSES, UNITS], U8, align_bytes=64)
        nc.vector.memset(base_scales[:].rearrange("p c n -> p (c n)").bitcast(I32), 0)
        scale_rows = base_weight_scales.rearrange("c q n -> q c n")
        for quadrant in range(4):
            nc.sync.dma_start(
                out=base_scales[32 * quadrant : 32 * quadrant + 4].bitcast(I32),
                in_=scale_rows[4 * quadrant : 4 * quadrant + 4].bitcast(I32),
            )

        w_rows = keep.tile([P, PASSES, PACK, UNITS * SLICES], BF16)
        nc.sync.dma_start(
            out=w_rows[:],
            in_=spline_weight.rearrange("(c p t) u s -> p c t (u s)", p=P, t=PACK),
        )
        for n in range(1, BLOCKS):
            nc.sync.dma_start(out=x_rows[n][:], in_=x_blocks[n])

        identity = keep.tile([P, P], F32)
        make_identity(nc, identity[:])

        w_grouped = keep.tile([P, GROUPS, PASSES, UNITS, PACK], BF16, align_bytes=64)
        w_codes = keep.tile([P, GROUPS, PASSES, UNITS], U32, align_bytes=64)
        w_scales = keep.tile([P, GROUPS, PASSES, UNITS], U8, align_bytes=64)
        w_by_slice = w_rows[:].rearrange("p c t (u s) -> p s c u t", s=SLICES)

        def regroup_weight(g):
            nc.gpsimd.tensor_scalar(
                out=w_grouped[:, g], in0=w_by_slice[:, g], scalar1=1.0, scalar2=0.0, op0=ALU.mult, op1=ALU.add
            )

        def quantise_weight(g):
            nc.vector.quantize_mx(
                out=w_codes[:, g].rearrange("p c u -> p (c u)").bitcast(FP8X4),
                scales=w_scales[:, g].rearrange("p c u -> p (c u)"),
                in_=w_grouped[:, g].rearrange("p c u t -> p (c u t)"),
            )

        def quantise_block(values, pool, groups_of_tiles=1):
            codes = pool.tile([P, TILES, PASSES, P], U32, align_bytes=64, name="codes")
            scales = pool.tile([P, TILES, PASSES, P], U8, align_bytes=64, name="scales")
            step = TILES // groups_of_tiles
            for j in range(0, TILES, step):
                nc.vector.quantize_mx(
                    out=codes[:, j : j + step].rearrange("p j c r -> p (j c r)").bitcast(FP8X4),
                    scales=scales[:, j : j + step].rearrange("p j c r -> p (j c r)"),
                    in_=values[:, j * TILE_COLS : (j + step) * TILE_COLS],
                )
            return codes, scales

        def multiply(acc, codes, scales, j, weight_codes, weight_scales, first, last):
            for c in range(PASSES):
                nc.tensor.matmul_mx(
                    out=acc,
                    lhsT=codes[:, j, c, :].bitcast(FP8X4),
                    lhsT_scale=scales[:, j, c, :],
                    rhs=weight_codes[:, c, :].bitcast(FP8X4),
                    rhs_scale=weight_scales[:, c, :],
                    start=(first and c == 0),
                    stop=(last and c == PASSES - 1),
                )

        x_banks, x_grouped, base_sum, tanh_half, twice_silu, spline_sum = {}, {}, {}, {}, {}, {}
        distance, rbf, rbf_coded = {}, {}, {}

        def transpose_piece(n, j, c):
            first_word = c * K_PASS // 2
            for u in range(PAIRS):
                nc.tensor.transpose(
                    x_banks[n][j][:, c, :, u],
                    x_rows[n][:].bitcast(F32)[:, j, first_word + u : first_word + K_PASS // 2 : PAIRS],
                    identity[:],
                )

        def new_banks(n):
            x_banks[n] = [x_psum.tile([P, PASSES, P, PAIRS], F32, name="x_bank") for j in range(TILES)]

        def transpose_block(n):
            new_banks(n)
            for j in range(TILES):
                for c in range(PASSES):
                    transpose_piece(n, j, c)

        def group_piece(n, j, passes):
            nc.vector.tensor_copy(
                out=x_grouped[n][:, piece_cols(j, passes)].bitcast(F32),
                in_=x_banks[n][j][:, passes, :, :].rearrange("p c r u -> p (c r u)"),
            )

        def piece_cols(j, passes):
            return slice(j * TILE_COLS + passes.start * P * PACK, j * TILE_COLS + passes.stop * P * PACK)

        def new_grouped(n):
            x_grouped[n] = by_block.tile([P, BLOCK_COLS], BF16, align_bytes=64, name="x_grouped")

        def group_block(n):
            new_grouped(n)
            for j in range(TILES):
                group_piece(n, j, slice(0, PASSES))

        def gpsimd_distance(n):
            middle = distances.tile([P, BLOCK_COLS], F32)
            for j in range(TILES):
                cols = slice(j * TILE_COLS, (j + 1) * TILE_COLS)
                nc.gpsimd.tensor_tensor(
                    out=middle[:, cols], in0=x_grouped[n][:, cols], in1=x_grouped[n][:, cols], op=ALU.mult
                )
            distance[n, ON_GPSIMD] = middle
            if n in SHARED_BLOCKS:
                distance[n, SHARED] = distances.tile([P, BLOCK_COLS], F32, name="distance%d" % SHARED)
                first = slice(0, TILE_COLS)
                nc.gpsimd.tensor_tensor(
                    out=distance[n, SHARED][:, first], in0=middle[:, first], in1=x_grouped[n][:, first], op=ALU.subtract
                )

        def vector_distance(n, g):
            shared = g == SHARED and n in SHARED_BLOCKS
            if not shared:
                distance[n, g] = distances.tile([P, BLOCK_COLS], F32, name="distance%d" % g)
            for j in range(1 if shared else 0, TILES):
                cols = slice(j * TILE_COLS, (j + 1) * TILE_COLS)
                nc.vector.scalar_tensor_tensor(
                    out=distance[n, g][:, cols],
                    in0=x_banks[n][j][:].rearrange("p c r u -> p (c r u)").bitcast(BF16),
                    scalar=2.0 * CENTRES[g],
                    in1=x_grouped[n][:, cols],
                    op0=ALU.subtract,
                    op1=ALU.mult,
                )

        def scalar_distance(n, cols):
            if cols.start == 0:
                distance[n, ON_SCALAR] = distances.tile([P, BLOCK_COLS], F32, name="distance%d" % ON_SCALAR)
            nc.scalar.activation(
                out=distance[n, ON_SCALAR][:, cols], in_=x_grouped[n][:, cols], func=ACT.Square, bias=-CENTRES[ON_SCALAR]
            )

        def exponential(n, g, left_out, pieces=1):
            rbf[n, g] = rbfs.tile([P, BLOCK_COLS], BF16, align_bytes=64, name="rbf")
            width = BLOCK_COLS // pieces
            for first_col in range(0, BLOCK_COLS, width):
                nc.scalar.activation(
                    out=rbf[n, g][:, first_col : first_col + width],
                    in_=distance[n, g][:, first_col : first_col + width],
                    func=ACT.Exp,
                    scale=-SHARPNESS,
                    bias=-SHARPNESS * left_out,
                )

        def base_product(n):
            x_codes, x_scales = quantise_block(x_grouped[n][:], coded)
            base_sum[n] = sums.tile([P, TILES, UNITS], F32, name="base_sum")
            for j in range(TILES):
                multiply(base_sum[n][:, j, :], x_codes, x_scales, j, base_codes, base_scales, True, True)

        def tanh_block(n):
            tanh_half[n] = by_block.tile([P, TILES * UNITS], F32, name="tanh_half")
            nc.scalar.activation(
                out=tanh_half[n][:], in_=base_sum[n][:].rearrange("p j u -> p (j u)"), func=ACT.Tanh, scale=0.5
            )

        def silu_block(n):
            twice_silu[n] = silus.tile([P, TILES, UNITS], F32, name="twice_silu")
            nc.vector.scalar_tensor_tensor(
                out=twice_silu[n][:].rearrange("p j u -> p (j u)"),
                in0=tanh_half[n][:],
                scalar=1.0,
                in1=base_sum[n][:].rearrange("p j u -> p (j u)"),
                op0=ALU.add,
                op1=ALU.mult,
            )

        def quantise_rbf(n, g, groups_of_tiles=1):
            rbf_coded[n, g] = quantise_block(rbf[n, g][:], waiting, groups_of_tiles)

        def open_sums(n):
            if n == BLOCKS - 1:
                spline_sum[n] = [spline_sums.tile([P, UNITS], F32, name="spline_sum") for j in range(TILES)]
            else:
                spline_sum[n] = [spline_sums.tile([P, TILES, UNITS], F32, name="spline_sum")]

        def product(n, g, j):
            acc = spline_sum[n][j][:] if n == BLOCKS - 1 else spline_sum[n][0][:, j, :]
            rbf_codes, rbf_scales = rbf_coded[n, g]
            multiply(
                acc, rbf_codes, rbf_scales, j, w_codes[:, g], w_scales[:, g],
                g == ROUND_ORDER[0], g == ROUND_ORDER[-1],
            )

        def products(n):
            open_sums(n)
            for j in range(TILES):
                for g in ROUND_ORDER:
                    product(n, g, j)

        def finish_block(n):
            result = by_block.tile([P, TILES, UNITS], F32)
            if n == BLOCKS - 1:
                for j in range(TILES):
                    nc.vector.scalar_tensor_tensor(
                        out=result[:, j, :], in0=twice_silu[n][:, j, :], scalar=0.5, in1=spline_sum[n][j][:],
                        op0=ALU.mult, op1=ALU.add,
                    )
                    nc.sync.dma_start(out=out_blocks[n][:, j, :], in_=result[:, j, :])
            else:
                nc.vector.scalar_tensor_tensor(
                    out=result[:].rearrange("p j u -> p (j u)"),
                    in0=twice_silu[n][:].rearrange("p j u -> p (j u)"),
                    scalar=0.5,
                    in1=spline_sum[n][0][:].rearrange("p j u -> p (j u)"),
                    op0=ALU.mult,
                    op1=ALU.add,
                )
                nc.sync.dma_start(out=out_blocks[n], in_=result[:])

        new_banks(0)
        new_grouped(0)
        for c in range(PASSES):
            for j in range(TILES):
                transpose_piece(0, j, c)
                group_piece(0, j, slice(c, c + 1))
        for c in range(PASSES):
            for j in range(TILES):
                scalar_distance(0, piece_cols(j, slice(c, c + 1)))
        complete = []
        multiplied = []

        def last_quantise(n):
            quantise_rbf(n, round_order(n)[-1])
            complete.append(n)

        def multiply_complete_blocks():
            for n in complete:
                products(n)
                multiplied.append(n)
            complete.clear()

        for k in range(-1, BLOCKS):
            if k == BLOCKS - 1:
                last_quantise(k - 1)
                multiply_complete_blocks()
            if k + 1 < BLOCKS:
                if k + 1 > 0:
                    group_block(k + 1)
                gpsimd_distance(k + 1)
            for n, g in JUST_IN_TIME:
                if n == k:
                    vector_distance(n, g)
            for g in REGROUP_IN_ROUND.get(k, ()):
                regroup_weight(g)
            if k + 1 < BLOCKS:
                for g in ON_VECTOR + (() if k + 1 in SCALAR_BLOCKS else (ON_SCALAR,)):
                    if (k + 1, g) not in JUST_IN_TIME:
                        vector_distance(k + 1, g)
            for n in multiplied:
                finish_block(n)
            multiplied.clear()
            if k > 0 and k in SCALAR_BLOCKS:
                scalar_distance(k, slice(0, BLOCK_COLS))
            if k >= 0:
                for g in round_order(k):
                    by_square = g == ON_SCALAR and k in SCALAR_BLOCKS
                    pieces = TILES if (k == BLOCKS - 1 and g == ROUND_ORDER[-1]) else 1
                    exponential(k, g, 0.0 if by_square else CENTRES[g] * CENTRES[g], pieces)
                    if g == (3 if k == 0 else round_order(k)[0]):
                        tanh_block(k)
                silu_block(k)
            if k + 2 < BLOCKS:
                transpose_block(k + 2)
            if 1 <= k < BLOCKS - 1:
                last_quantise(k - 1)
            if k + 1 < BLOCKS:
                base_product(k + 1)
            if k == WEIGHTS_ROUND:
                for g in ROUND_ORDER:
                    quantise_weight(g)
            if WEIGHTS_ROUND <= k < BLOCKS - 1:
                multiply_complete_blocks()
            if k == BLOCKS - 1:
                open_sums(k)
                for g in ROUND_ORDER:
                    quantise_rbf(k, g, TILES if g == ROUND_ORDER[-1] else 1)
                    for j in range(TILES):
                        product(k, g, j)
            elif k >= 0:
                for g in round_order(k)[:-1]:
                    quantise_rbf(k, g)
        finish_block(BLOCKS - 1)
